import numpy as np
import ml_dtypes


def mxq(x, axis, fmt="e4m3"):
    dtype, down = {"e4m3": (ml_dtypes.float8_e4m3fn, 7), "e5m2": (ml_dtypes.float8_e5m2, 14)}[fmt]
    v = np.moveaxis(np.asarray(x, np.float32).astype(ml_dtypes.bfloat16).astype(np.float64), axis, -1)
    blocks = v.reshape(v.shape[:-1] + (-1, 32))
    amax = np.abs(blocks).max(-1, keepdims=True)
    byte = np.maximum(np.where(amax > 0, np.frexp(amax)[1] - 1 + 127, 0) - down, 1)
    scale = np.exp2(byte - 127.0)
    codes = (blocks / scale).astype(np.float32).astype(dtype).astype(np.float64)
    return np.moveaxis((codes * scale).reshape(v.shape), -1, axis)


WIDE = False


def mx_kscale(k):
    if not WIDE:
        return np.ones(k)
    levels = np.array([10, -10, 5, -5, 0])
    if k % 512:
        return np.exp2(np.random.permutation(np.resize(levels, k // 32))).repeat(32)
    a = np.empty((k // 512, 16))
    for p in range(k // 512):
        a[p, :8] = np.random.permutation(np.resize(levels, 8))
        for g in range(8):
            far = levels[np.abs(levels - a[p, g]) >= 10]
            a[p, g + 8] = far[np.random.randint(len(far))]
    return np.exp2(a.ravel()).repeat(32)


BF16 = ml_dtypes.bfloat16


def bf(x):
    return np.asarray(x, np.float32).astype(BF16)


def f64(x):
    return np.asarray(x).astype(np.float64)


B, S, D, H = 1, 1024, 512, 512


def setup_inputs():
    s, t = mx_kscale(D), mx_kscale(H)
    return {"audio_feature": bf(np.random.standard_normal((B, S, D)) * s),
            "W_phi": bf(np.random.standard_normal((D, H)) / np.sqrt(D) / s[:, None] * t),
            "b_phi": bf(np.random.standard_normal(H) * 0.2 * t),
            "W_theta": bf(np.random.standard_normal((D, H)) / np.sqrt(D) / s[:, None] / t),
            "b_theta": bf(np.random.standard_normal(H) * 0.2 / t)}


def reference(audio_feature, W_phi, b_phi, W_theta, b_theta):
    xq = mxq(f64(audio_feature), 2, "e4m3")
    phi_a = f64(bf(xq @ mxq(f64(W_phi), 0, "e4m3"))) + f64(b_phi)
    theta_a = f64(bf(xq @ mxq(f64(W_theta), 0, "e4m3"))) + f64(b_theta)
    scores = (mxq(phi_a, 2, "e4m3") @ mxq(theta_a, 2, "e4m3").transpose(0, 2, 1)) / np.sqrt(D)
    scores = np.maximum(scores, 0.0)
    return (scores + scores.transpose(0, 2, 1)) * 0.5

@@ -1,0 +1,259 @@
+from contextlib import ExitStack
+
+import math
+
+import concourse.mybir as mybir
+from concourse.masks import make_identity
+
+TOK, D_IN, HID = 1024, 512, 512
+FLOPS = 2 * TOK * D_IN * HID * 2 + 2 * TOK * TOK * HID
+
+F32 = mybir.dt.float32
+BF16 = mybir.dt.bfloat16
+U32 = mybir.dt.uint32
+U8 = mybir.dt.uint8
+FP8X4 = mybir.dt.float8_e4m3fn_x4
+ACT = mybir.ActivationFunctionType
+ALU = mybir.AluOpType
+
+P = 128
+PACK = 4
+NT = TOK // P
+BANK_DT = BF16
+OUT_SCALE = 0.5 / math.sqrt(D_IN)
+SG_UNITS = (1, 3, 5, 7)
+PIECES = {512: (512,), 384: (128, 256), 256: (256,), 128: (128,)}
+
+
+def tile_selfattention_pa_kernel(tc, audio_feature, W_phi, b_phi, W_theta, b_theta, out):
+    nc = tc.nc
+    x = audio_feature.flatten_outer_dims()
+    o2 = out.flatten_outer_dims()
+    w_dram = (W_theta, W_phi)
+    b_dram = (b_theta, b_phi)
+
+    with ExitStack() as ctx:
+        keep = ctx.enter_context(tc.tile_pool(name="keep", bufs=1))
+        work = ctx.enter_context(tc.tile_pool(name="work", bufs=3))
+        ps_a = ctx.enter_context(tc.psum_pool(name="ps_a", bufs=3))
+        ps_b = ctx.enter_context(tc.psum_pool(name="ps_b", bufs=5))
+
+        b_raw = []
+        for w in range(2):
+            br = keep.tile([P, PACK], BF16, name="b_raw%d" % w)
+            nc.scalar.dma_start(out=br[:], in_=b_dram[w].rearrange("(p t) -> p t", t=PACK))
+            b_raw.append(br)
+
+        w_raw = []
+        x_sb = []
+        for w in range(2):
+            wr = keep.tile([P, PACK, HID], BF16, name="w_raw%d" % w)
+            w_raw.append(wr)
+        for ch in range(4):
+            xc = keep.tile([P, 2, D_IN], BF16, name="x_sb%d" % ch)
+            x_sb.append(xc)
+
+        def load_w(w):
+            nc.sync.dma_start(out=w_raw[w][:], in_=w_dram[w].rearrange("(p j) c -> p j c", j=PACK))
+
+        def load_x(ch):
+            nc.sync.dma_start(
+                out=x_sb[ch][:],
+                in_=x[2 * P * ch : 2 * P * (ch + 1), :].rearrange("(n p) k -> p n k", p=P),
+            )
+
+        load_w(0)
+        load_x(0)
+        load_x(1)
+        load_w(1)
+        load_x(2)
+        load_x(3)
+
+        ident = keep.tile([P, P], F32, name="ident")
+        make_identity(nc, ident[:])
+        zero1 = keep.tile([P, 1], F32, name="zero1")
+        warm1 = keep.tile([P, 1], F32, name="warm1")
+        nc.vector.memset(zero1[:], 0.0)
+        nc.scalar.activation(out=warm1[:], in_=zero1[:], func=ACT.Relu)
+        bias = []
+        for w in range(2):
+            bf = keep.tile([P, PACK], F32, name="bias%d" % w)
+            nc.vector.tensor_copy(out=bf[:], in_=b_raw[w][:])
+            bias.append(bf)
+
+        xg = keep.tile([P, TOK * PACK], BF16, name="xg", align_bytes=64)
+        xq = keep.tile([P, TOK], U32, name="xq", align_bytes=64)
+        xs = keep.tile([P, TOK], U8, name="xs", align_bytes=64)
+        wg, wq, ws, hg, hq, hs = [], [], [], [], [], []
+        for w in range(2):
+            t_wg = keep.tile([P, HID * PACK], BF16, name="wg%d" % w, align_bytes=64)
+            t_wq = keep.tile([P, HID], U32, name="wq%d" % w, align_bytes=64)
+            t_ws = keep.tile([P, HID], U8, name="ws%d" % w, align_bytes=64)
+            t_hg = keep.tile([P, TOK * PACK], BF16, name="hg%d" % w, align_bytes=64)
+            t_hq = keep.tile([P, TOK], U32, name="hq%d" % w, align_bytes=64)
+            t_hs = keep.tile([P, TOK], U8, name="hs%d" % w, align_bytes=64)
+            wg.append(t_wg)
+            wq.append(t_wq)
+            ws.append(t_ws)
+            hg.append(t_hg)
+            hq.append(t_hq)
+            hs.append(t_hs)
+
+        def x_chunk(ch):
+            xt = ps_a.tile([P, 2, 2, P], F32, tag="A", name="xt")
+            for n2 in range(2):
+                words = x_sb[ch][:, n2, :].bitcast(F32)
+                for u in range(2):
+                    nc.tensor.transpose(xt[:, n2, u, :], words[:, u : D_IN // 2 : 2], ident[:])
+            nc.scalar.copy(
+                out=xg[:, 1024 * ch : 1024 * (ch + 1)].bitcast(F32).rearrange("p (n r u) -> p n r u", n=2, u=2),
+                in_=xt[:].rearrange("p n u r -> p n r u"),
+            )
+            nc.vector.quantize_mx(
+                out=xq[:, 256 * ch : 256 * (ch + 1)].bitcast(FP8X4),
+                scales=xs[:, 256 * ch : 256 * (ch + 1)],
+                in_=xg[:, 1024 * ch : 1024 * (ch + 1)],
+            )
+
+        def w_prep(w, shares):
+            dst = wg[w][:].rearrange("p (t m j) -> p t m j", t=PACK, j=PACK)
+            src = w_raw[w][:].rearrange("p j (m t) -> p t m j", t=PACK)
+            for eng, t0, t1 in shares:
+                if eng == "G":
+                    nc.gpsimd.tensor_scalar(
+                        out=dst[:, t0:t1], in0=src[:, t0:t1], scalar1=1.0, scalar2=0.0, op0=ALU.mult, op1=ALU.add
+                    )
+                elif eng == "S":
+                    nc.scalar.copy(out=dst[:, t0:t1], in_=src[:, t0:t1])
+                else:
+                    nc.vector.tensor_copy(out=dst[:, t0:t1], in_=src[:, t0:t1])
+            nc.vector.quantize_mx(out=wq[w][:].bitcast(FP8X4), scales=ws[w][:], in_=wg[w][:])
+
+        def unit(w, n):
+            ps1 = ps_a.tile([P, PACK, P], BANK_DT, tag="A", name="ps1")
+            for t in range(PACK):
+                nc.tensor.matmul_mx(
+                    out=ps1[:, t, :],
+                    lhsT=wq[w][:, P * t : P * (t + 1)].bitcast(FP8X4),
+                    lhsT_scale=ws[w][:, P * t : P * (t + 1)],
+                    rhs=xq[:, P * n : P * (n + 1)].bitcast(FP8X4),
+                    rhs_scale=xs[:, P * n : P * (n + 1)],
+                    start=True,
+                    stop=True,
+                )
+            dst = hg[w][:, 512 * n : 512 * (n + 1)].rearrange("p (r t) -> p r t", t=PACK)
+            if n in SG_UNITS:
+                lin = work.tile([P, PACK, P], BF16, tag="lin", name="lin", bufs=3)
+                for t in range(PACK):
+                    nc.scalar.activation(
+                        out=lin[:, t, :], in_=ps1[:, t, :], func=ACT.Identity, bias=bias[w][:, t : t + 1], scale=1.0
+                    )
+                nc.gpsimd.tensor_scalar(
+                    out=dst, in0=lin[:].rearrange("p t r -> p r t"), scalar1=1.0, scalar2=0.0, op0=ALU.mult, op1=ALU.add
+                )
+            else:
+                nc.vector.tensor_tensor(
+                    out=dst,
+                    in0=ps1[:].rearrange("p t r -> p r t"),
+                    in1=bias[w][:].unsqueeze(1).to_broadcast([P, P, PACK]),
+                    op=ALU.add,
+                )
+
+        def quant_pair(w, m):
+            nc.vector.quantize_mx(
+                out=hq[w][:, 256 * m : 256 * (m + 1)].bitcast(FP8X4),
+                scales=hs[w][:, 256 * m : 256 * (m + 1)],
+                in_=hg[w][:, 1024 * m : 1024 * (m + 1)],
+            )
+
+        def half(w, h):
+            for m in (2 * h, 2 * h + 1):
+                unit(w, 2 * m)
+                unit(w, 2 * m + 1)
+                quant_pair(w, m)
+
+        def mx2(dst, wl, i, wr, col0, width):
+            nc.tensor.matmul_mx(
+                out=dst,
+                lhsT=hq[wl][:, P * i : P * (i + 1)].bitcast(FP8X4),
+                lhsT_scale=hs[wl][:, P * i : P * (i + 1)],
+                rhs=hq[wr][:, col0 : col0 + width].bitcast(FP8X4),
+                rhs_scale=hs[wr][:, col0 : col0 + width],
+                start=True,
+                stop=True,
+            )
+
+        t_keep = {}
+        o_tiles = {}
+
+        def o_tile(i, c):
+            if (i, c) not in o_tiles:
+                o_sb = work.tile([P, 512], F32, tag="o_sb", name="o_sb", bufs=6)
+                o_tiles[(i, c)] = o_sb
+            return o_tiles[(i, c)]
+
+        def upper(i, c):
+            lo = max(0, P * i - 512 * c)
+            pa = ps_b.tile([P, 512], F32, tag="B", name="pa")
+            pb = ps_b.tile([P, 512], F32, tag="B", name="pb")
+            for dst, wl, wr in ((pa, 1, 0), (pb, 0, 1)):
+                col = lo
+                for width in PIECES[512 - lo]:
+                    mx2(dst[:, col : col + width], wl, i, wr, 512 * c + col, width)
+                    col += width
+            a_sb = work.tile([P, 512], F32, tag="a_sb", name="a_sb", bufs=4)
+            t_sb = keep.tile([P, 512], F32, name="t_sb%d%d" % (i, c))
+            t_keep[(i, c)] = t_sb
+            o_sb = o_tile(i, c)
+            nc.scalar.activation(out=a_sb[:, lo:], in_=pa[:, lo:], func=ACT.Relu)
+            nc.vector.scalar_tensor_tensor(
+                out=t_sb[:, lo:], in0=pb[:, lo:], scalar=0.0, in1=a_sb[:, lo:], op0=ALU.max, op1=ALU.add
+            )
+            nc.gpsimd.tensor_scalar(
+                out=o_sb[:, lo:], in0=t_sb[:, lo:], scalar1=OUT_SCALE, scalar2=0.0, op0=ALU.mult, op1=ALU.add
+            )
+
+        def lower(i, c, on_vector):
+            nblk = min(4, i - 4 * c)
+            pt = ps_b.tile([P, 512], F32, tag="B", name="pt")
+            ci = i // 4
+            for q in range(nblk):
+                src = t_keep[(4 * c + q, ci)]
+                nc.tensor.transpose(pt[:, P * q : P * (q + 1)], src[:, P * (i - 4 * ci) : P * (i - 4 * ci + 1)], ident[:])
+            o_sb = o_tile(i, c)
+            if on_vector:
+                nc.vector.tensor_scalar_mul(out=o_sb[:, : P * nblk], in0=pt[:, : P * nblk], scalar1=OUT_SCALE)
+            else:
+                nc.scalar.activation(out=o_sb[:, : P * nblk], in_=pt[:, : P * nblk], func=ACT.Copy, scale=OUT_SCALE)
+
+        def store(i, c):
+            nc.sync.dma_start(out=o2[P * i : P * (i + 1), 512 * c : 512 * (c + 1)], in_=o_tiles[(i, c)][:])
+
+        w_prep(0, (("V", 0, 2), ("G", 2, 3), ("S", 3, 4)))
+        x_chunk(0)
+        x_chunk(1)
+        w_prep(1, (("V", 0, 1), ("G", 1, 3), ("S", 3, 4)))
+        x_chunk(2)
+        x_chunk(3)
+        half(0, 0)
+        half(1, 0)
+        half(0, 1)
+        half(1, 1)
+        for i in range(4):
+            upper(i, 0)
+        store(0, 0)
+        for i in range(1, 4):
+            lower(i, 0, False)
+            store(i, 0)
+        for i in range(4):
+            upper(i, 1)
+            store(i, 1)
+        for i in range(4, 8):
+            lower(i, 0, i % 2 == 0)
+            store(i, 0)
+        for i in range(4, 8):
+            upper(i, 1)
+        store(4, 1)
+        for i in range(5, 8):
+            lower(i, 1, i % 2 == 1)
+            store(i, 1)

@@ -21,8 +21,6 @@ PACK = 4
 NT = TOK // P
 BANK_DT = BF16
 OUT_SCALE = 0.5 / math.sqrt(D_IN)
-SG_UNITS = (1, 3, 5, 7)
-PIECES = {512: (512,), 384: (128, 256), 256: (256,), 128: (128,)}
 
 
 def tile_selfattention_pa_kernel(tc, audio_feature, W_phi, b_phi, W_theta, b_theta, out):
@@ -75,11 +73,7 @@ def tile_selfattention_pa_kernel(tc, audio_feature, W_phi, b_phi, W_theta, b_the
         warm1 = keep.tile([P, 1], F32, name="warm1")
         nc.vector.memset(zero1[:], 0.0)
         nc.scalar.activation(out=warm1[:], in_=zero1[:], func=ACT.Relu)
-        bias = []
-        for w in range(2):
-            bf = keep.tile([P, PACK], F32, name="bias%d" % w)
-            nc.vector.tensor_copy(out=bf[:], in_=b_raw[w][:])
-            bias.append(bf)
+        bias = b_raw
 
         xg = keep.tile([P, TOK * PACK], BF16, name="xg", align_bytes=64)
         xq = keep.tile([P, TOK], U32, name="xq", align_bytes=64)
@@ -129,21 +123,21 @@ def tile_selfattention_pa_kernel(tc, audio_feature, W_phi, b_phi, W_theta, b_the
                     nc.vector.tensor_copy(out=dst[:, t0:t1], in_=src[:, t0:t1])
             nc.vector.quantize_mx(out=wq[w][:].bitcast(FP8X4), scales=ws[w][:], in_=wg[w][:])
 
-        def unit(w, n):
-            ps1 = ps_a.tile([P, PACK, P], BANK_DT, tag="A", name="ps1")
+        def unit(w, m):
+            ps1 = ps_a.tile([P, PACK, 2 * P], BANK_DT, tag="A", name="ps1")
             for t in range(PACK):
                 nc.tensor.matmul_mx(
                     out=ps1[:, t, :],
                     lhsT=wq[w][:, P * t : P * (t + 1)].bitcast(FP8X4),
                     lhsT_scale=ws[w][:, P * t : P * (t + 1)],
-                    rhs=xq[:, P * n : P * (n + 1)].bitcast(FP8X4),
-                    rhs_scale=xs[:, P * n : P * (n + 1)],
+                    rhs=xq[:, 256 * m : 256 * (m + 1)].bitcast(FP8X4),
+                    rhs_scale=xs[:, 256 * m : 256 * (m + 1)],
                     start=True,
                     stop=True,
                 )
-            dst = hg[w][:, 512 * n : 512 * (n + 1)].rearrange("p (r t) -> p r t", t=PACK)
-            if n in SG_UNITS:
-                lin = work.tile([P, PACK, P], BF16, tag="lin", name="lin", bufs=3)
+            dst = hg[w][:, 1024 * m : 1024 * (m + 1)].rearrange("p (r t) -> p r t", t=PACK)
+            if w == 0 and m > 0:
+                lin = work.tile([P, PACK, 2 * P], BF16, tag="lin", name="lin", bufs=3)
                 for t in range(PACK):
                     nc.scalar.activation(
                         out=lin[:, t, :], in_=ps1[:, t, :], func=ACT.Identity, bias=bias[w][:, t : t + 1], scale=1.0
@@ -155,7 +149,7 @@ def tile_selfattention_pa_kernel(tc, audio_feature, W_phi, b_phi, W_theta, b_the
                 nc.vector.tensor_tensor(
                     out=dst,
                     in0=ps1[:].rearrange("p t r -> p r t"),
-                    in1=bias[w][:].unsqueeze(1).to_broadcast([P, P, PACK]),
+                    in1=bias[w][:].unsqueeze(1).to_broadcast([P, 2 * P, PACK]),
                     op=ALU.add,
                 )
 
@@ -165,12 +159,6 @@ def tile_selfattention_pa_kernel(tc, audio_feature, W_phi, b_phi, W_theta, b_the
                 scales=hs[w][:, 256 * m : 256 * (m + 1)],
                 in_=hg[w][:, 1024 * m : 1024 * (m + 1)],
             )
-
-        def half(w, h):
-            for m in (2 * h, 2 * h + 1):
-                unit(w, 2 * m)
-                unit(w, 2 * m + 1)
-                quant_pair(w, m)
 
         def mx2(dst, wl, i, wr, col0, width):
             nc.tensor.matmul_mx(
@@ -184,76 +172,71 @@ def tile_selfattention_pa_kernel(tc, audio_feature, W_phi, b_phi, W_theta, b_the
             )
 
         t_keep = {}
-        o_tiles = {}
 
-        def o_tile(i, c):
-            if (i, c) not in o_tiles:
-                o_sb = work.tile([P, 512], F32, tag="o_sb", name="o_sb", bufs=6)
-                o_tiles[(i, c)] = o_sb
-            return o_tiles[(i, c)]
-
-        def upper(i, c):
-            lo = max(0, P * i - 512 * c)
+        def direct(i, col0, width):
             pa = ps_b.tile([P, 512], F32, tag="B", name="pa")
             pb = ps_b.tile([P, 512], F32, tag="B", name="pb")
-            for dst, wl, wr in ((pa, 1, 0), (pb, 0, 1)):
-                col = lo
-                for width in PIECES[512 - lo]:
-                    mx2(dst[:, col : col + width], wl, i, wr, 512 * c + col, width)
-                    col += width
+            mx2(pa[:, :width], 1, i, 0, col0, width)
+            mx2(pb[:, :width], 0, i, 1, col0, width)
             a_sb = work.tile([P, 512], F32, tag="a_sb", name="a_sb", bufs=4)
-            t_sb = keep.tile([P, 512], F32, name="t_sb%d%d" % (i, c))
-            t_keep[(i, c)] = t_sb
-            o_sb = o_tile(i, c)
-            nc.scalar.activation(out=a_sb[:, lo:], in_=pa[:, lo:], func=ACT.Relu)
+            t_sb = keep.tile([P, 512], F32, name="t_sb%d_%d" % (i, col0))
+            t_keep[(i, col0 // 512)] = t_sb
+            o_sb = work.tile([P, 512], F32, tag="o_sb", name="o_sb", bufs=12)
+            nc.scalar.activation(out=a_sb[:, :width], in_=pa[:, :width], func=ACT.Relu)
             nc.vector.scalar_tensor_tensor(
-                out=t_sb[:, lo:], in0=pb[:, lo:], scalar=0.0, in1=a_sb[:, lo:], op0=ALU.max, op1=ALU.add
+                out=t_sb[:, :width], in0=pb[:, :width], scalar=0.0, in1=a_sb[:, :width], op0=ALU.max, op1=ALU.add
             )
-            nc.gpsimd.tensor_scalar(
-                out=o_sb[:, lo:], in0=t_sb[:, lo:], scalar1=OUT_SCALE, scalar2=0.0, op0=ALU.mult, op1=ALU.add
-            )
-
-        def lower(i, c, on_vector):
-            nblk = min(4, i - 4 * c)
-            pt = ps_b.tile([P, 512], F32, tag="B", name="pt")
-            ci = i // 4
-            for q in range(nblk):
-                src = t_keep[(4 * c + q, ci)]
-                nc.tensor.transpose(pt[:, P * q : P * (q + 1)], src[:, P * (i - 4 * ci) : P * (i - 4 * ci + 1)], ident[:])
-            o_sb = o_tile(i, c)
-            if on_vector:
-                nc.vector.tensor_scalar_mul(out=o_sb[:, : P * nblk], in0=pt[:, : P * nblk], scalar1=OUT_SCALE)
+            if i >= NT - 2:
+                nc.vector.tensor_scalar_mul(out=o_sb[:, :width], in0=t_sb[:, :width], scalar1=OUT_SCALE)
             else:
-                nc.scalar.activation(out=o_sb[:, : P * nblk], in_=pt[:, : P * nblk], func=ACT.Copy, scale=OUT_SCALE)
+                nc.gpsimd.tensor_scalar(
+                    out=o_sb[:, :width], in0=t_sb[:, :width], scalar1=OUT_SCALE, scalar2=0.0, op0=ALU.mult, op1=ALU.add
+                )
+            nc.sync.dma_start(out=o2[P * i : P * (i + 1), col0 : col0 + width], in_=o_sb[:, :width])
 
-        def store(i, c):
-            nc.sync.dma_start(out=o2[P * i : P * (i + 1), 512 * c : 512 * (c + 1)], in_=o_tiles[(i, c)][:])
+        def mirror(g, jp, on_vector):
+            pt = ps_b.tile([P, 2, 2, P], F32, tag="B", name="pt")
+            for jj in range(2):
+                j = 2 * jp + jj
+                for ii in range(2):
+                    t_sb = t_keep[(2 * g + ii, j // 4)]
+                    nc.tensor.transpose(pt[:, jj, ii, :], t_sb[:, P * (j % 4) : P * (j % 4 + 1)], ident[:])
+            m_sb = work.tile([P, 2, 2 * P], F32, tag="o_sb", name="m_sb", bufs=12)
+            flat = pt[:].rearrange("p a b r -> p (a b r)")
+            if on_vector:
+                nc.vector.tensor_scalar_mul(out=m_sb[:].rearrange("p a c -> p (a c)"), in0=flat, scalar1=OUT_SCALE)
+            else:
+                nc.scalar.activation(out=m_sb[:].rearrange("p a c -> p (a c)"), in_=flat, func=ACT.Copy, scale=OUT_SCALE)
+            nc.sync.dma_start(
+                out=o2[256 * jp : 256 * (jp + 1), 256 * g : 256 * (g + 1)].rearrange("(a p) c -> p a c", p=P),
+                in_=m_sb[:],
+            )
+
+        def group1(g):
+            unit(0, g)
+            unit(1, g)
+            quant_pair(1, g)
+            quant_pair(0, g)
+
+        def stage2(g):
+            width = 256 * (g + 1)
+            for i in (2 * g, 2 * g + 1):
+                for col0 in range(0, width, 512):
+                    direct(i, col0, min(512, width - col0))
+            for jp in range(g):
+                mirror(g, jp, jp % 2 == 1)
 
         w_prep(0, (("V", 0, 2), ("G", 2, 3), ("S", 3, 4)))
         x_chunk(0)
         x_chunk(1)
         w_prep(1, (("V", 0, 1), ("G", 1, 3), ("S", 3, 4)))
+        group1(0)
         x_chunk(2)
+        group1(1)
+        stage2(0)
         x_chunk(3)
-        half(0, 0)
-        half(1, 0)
-        half(0, 1)
-        half(1, 1)
-        for i in range(4):
-            upper(i, 0)
-        store(0, 0)
-        for i in range(1, 4):
-            lower(i, 0, False)
-            store(i, 0)
-        for i in range(4):
-            upper(i, 1)
-            store(i, 1)
-        for i in range(4, 8):
-            lower(i, 0, i % 2 == 0)
-            store(i, 0)
-        for i in range(4, 8):
-            upper(i, 1)
-        store(4, 1)
-        for i in range(5, 8):
-            lower(i, 1, i % 2 == 1)
-            store(i, 1)
+        group1(2)
+        stage2(1)
+        group1(3)
+        stage2(2)
+        stage2(3)

@@ -171,43 +171,53 @@ def tile_selfattention_pa_kernel(tc, audio_feature, W_phi, b_phi, W_theta, b_the
                 stop=True,
             )
 
-        t_keep = {}
+        t_loc = {}
 
-        def direct(i, col0, width):
+        def direct(pieces, on_vector):
             pa = ps_b.tile([P, 512], F32, tag="B", name="pa")
             pb = ps_b.tile([P, 512], F32, tag="B", name="pb")
-            mx2(pa[:, :width], 1, i, 0, col0, width)
-            mx2(pb[:, :width], 0, i, 1, col0, width)
+            t_sb = keep.tile([P, 512], F32, name="t_sb%d_%d" % (pieces[0][0], pieces[0][1]))
+            off = 0
+            for i, col0, width in pieces:
+                mx2(pa[:, off : off + width], 1, i, 0, col0, width)
+                for b in range(width // P):
+                    t_loc[(i, col0 // P + b)] = (t_sb, off + P * b)
+                off += width
+            off = 0
+            for i, col0, width in pieces:
+                mx2(pb[:, off : off + width], 0, i, 1, col0, width)
+                off += width
             a_sb = work.tile([P, 512], F32, tag="a_sb", name="a_sb", bufs=4)
-            t_sb = keep.tile([P, 512], F32, name="t_sb%d_%d" % (i, col0))
-            t_keep[(i, col0 // 512)] = t_sb
             o_sb = work.tile([P, 512], F32, tag="o_sb", name="o_sb", bufs=12)
-            nc.scalar.activation(out=a_sb[:, :width], in_=pa[:, :width], func=ACT.Relu)
-            nc.vector.scalar_tensor_tensor(
-                out=t_sb[:, :width], in0=pb[:, :width], scalar=0.0, in1=a_sb[:, :width], op0=ALU.max, op1=ALU.add
-            )
-            if i >= NT - 2:
-                nc.vector.tensor_scalar_mul(out=o_sb[:, :width], in0=t_sb[:, :width], scalar1=OUT_SCALE)
+            nc.scalar.activation(out=a_sb[:], in_=pa[:], func=ACT.Relu)
+            nc.vector.scalar_tensor_tensor(out=t_sb[:], in0=pb[:], scalar=0.0, in1=a_sb[:], op0=ALU.max, op1=ALU.add)
+            if on_vector:
+                nc.vector.tensor_scalar_mul(out=o_sb[:], in0=t_sb[:], scalar1=OUT_SCALE)
             else:
-                nc.gpsimd.tensor_scalar(
-                    out=o_sb[:, :width], in0=t_sb[:, :width], scalar1=OUT_SCALE, scalar2=0.0, op0=ALU.mult, op1=ALU.add
+                nc.gpsimd.tensor_scalar(out=o_sb[:], in0=t_sb[:], scalar1=OUT_SCALE, scalar2=0.0, op0=ALU.mult, op1=ALU.add)
+            i, col0, width = pieces[0]
+            if len(pieces) == 1:
+                nc.sync.dma_start(out=o2[P * i : P * (i + 1), col0 : col0 + width], in_=o_sb[:])
+            else:
+                nc.sync.dma_start(
+                    out=o2[P * i : P * (i + 2), col0 : col0 + width].rearrange("(a p) c -> p a c", p=P),
+                    in_=o_sb[:].rearrange("p (a c) -> p a c", a=2),
                 )
-            nc.sync.dma_start(out=o2[P * i : P * (i + 1), col0 : col0 + width], in_=o_sb[:, :width])
 
         def mirror(g, jp, on_vector):
             pt = ps_b.tile([P, 2, 2, P], F32, tag="B", name="pt")
             for jj in range(2):
-                j = 2 * jp + jj
                 for ii in range(2):
-                    t_sb = t_keep[(2 * g + ii, j // 4)]
-                    nc.tensor.transpose(pt[:, jj, ii, :], t_sb[:, P * (j % 4) : P * (j % 4 + 1)], ident[:])
+                    t_sb, off = t_loc[(2 * g + ii, 2 * jp + jj)]
+                    nc.tensor.transpose(pt[:, jj, ii, :], t_sb[:, off : off + P], ident[:])
             m_sb = work.tile([P, 2, 2 * P], F32, tag="o_sb", name="m_sb", bufs=12)
             flat = pt[:].rearrange("p a b r -> p (a b r)")
             if on_vector:
                 nc.vector.tensor_scalar_mul(out=m_sb[:].rearrange("p a c -> p (a c)"), in0=flat, scalar1=OUT_SCALE)
             else:
                 nc.scalar.activation(out=m_sb[:].rearrange("p a c -> p (a c)"), in_=flat, func=ACT.Copy, scale=OUT_SCALE)
-            nc.sync.dma_start(
+            queue = nc.sync if on_vector else nc.scalar
+            queue.dma_start(
                 out=o2[256 * jp : 256 * (jp + 1), 256 * g : 256 * (g + 1)].rearrange("(a p) c -> p a c", p=P),
                 in_=m_sb[:],
             )
@@ -219,10 +229,18 @@ def tile_selfattention_pa_kernel(tc, audio_feature, W_phi, b_phi, W_theta, b_the
             quant_pair(0, g)
 
         def stage2(g):
-            width = 256 * (g + 1)
-            for i in (2 * g, 2 * g + 1):
-                for col0 in range(0, width, 512):
-                    direct(i, col0, min(512, width - col0))
+            rows = (2 * g, 2 * g + 1)
+            last = g == NT // 2 - 1
+            for col0 in range(0, 512 * (g // 2), 512):
+                for i in rows:
+                    direct(((i, col0, 512),), False)
+            if g % 2 == 1 and not last:
+                for i in rows:
+                    direct(((i, 256 * (g - 1), 512),), False)
+            if g % 2 == 1 and last:
+                direct(tuple((i, 256 * (g - 1), 256) for i in rows), False)
+            if g % 2 == 0 or last:
+                direct(tuple((i, 256 * g, 256) for i in rows), last)
             for jp in range(g):
                 mirror(g, jp, jp % 2 == 1)
 

@@ -21,6 +21,7 @@ PACK = 4
 NT = TOK // P
 BANK_DT = BF16
 OUT_SCALE = 0.5 / math.sqrt(D_IN)
+N_HEAT = 4
 
 
 def tile_selfattention_pa_kernel(tc, audio_feature, W_phi, b_phi, W_theta, b_theta, out):
@@ -74,6 +75,16 @@ def tile_selfattention_pa_kernel(tc, audio_feature, W_phi, b_phi, W_theta, b_the
         nc.vector.memset(zero1[:], 0.0)
         nc.scalar.activation(out=warm1[:], in_=zero1[:], func=ACT.Relu)
         bias = b_raw
+
+        heat = keep.tile([P, 512], BF16, name="heat")
+        nc.gpsimd.memset(heat[:], 0.0)
+        hot = ps_b.tile([P, 512], F32, tag="B", name="hot")
+
+        def dummy(moving, times):
+            for rep in range(times):
+                nc.tensor.matmul(out=hot[:], lhsT=heat[:, :P], rhs=moving, start=True, stop=True)
+
+        dummy(heat[:], N_HEAT)
 
         xg = keep.tile([P, TOK * PACK], BF16, name="xg", align_bytes=64)
         xq = keep.tile([P, TOK], U32, name="xq", align_bytes=64)
@@ -244,9 +255,12 @@ def tile_selfattention_pa_kernel(tc, audio_feature, W_phi, b_phi, W_theta, b_the
             for jp in range(g):
                 mirror(g, jp, jp % 2 == 1)
 
+        dummy(w_raw[0][:, 0, :], 2)
         w_prep(0, (("V", 0, 2), ("G", 2, 3), ("S", 3, 4)))
         x_chunk(0)
+        dummy(x_sb[0][:, 0, :], 2)
         x_chunk(1)
+        dummy(x_sb[1][:, 0, :], 2)
         w_prep(1, (("V", 0, 1), ("G", 1, 3), ("S", 3, 4)))
         group1(0)
         x_chunk(2)

@@ -62,9 +62,9 @@ def tile_selfattention_pa_kernel(tc, audio_feature, W_phi, b_phi, W_theta, b_the
             )
 
         load_w(0)
+        load_w(1)
         load_x(0)
         load_x(1)
-        load_w(1)
         load_x(2)
         load_x(3)
 
@@ -77,7 +77,7 @@ def tile_selfattention_pa_kernel(tc, audio_feature, W_phi, b_phi, W_theta, b_the
         bias = b_raw
 
         heat = keep.tile([P, 512], BF16, name="heat")
-        nc.gpsimd.memset(heat[:], 0.0)
+        nc.vector.memset(heat[:], 0.0)
         hot = ps_b.tile([P, 512], F32, tag="B", name="hot")
 
         def dummy(moving, times):
@@ -256,12 +256,12 @@ def tile_selfattention_pa_kernel(tc, audio_feature, W_phi, b_phi, W_theta, b_the
                 mirror(g, jp, jp % 2 == 1)
 
         dummy(w_raw[0][:, 0, :], 2)
-        w_prep(0, (("V", 0, 2), ("G", 2, 3), ("S", 3, 4)))
+        w_prep(0, (("V", 0, 2), ("S", 2, 4)))
+        dummy(w_raw[1][:, 0, :], 2)
+        w_prep(1, (("V", 0, 2), ("S", 2, 4)))
         x_chunk(0)
         dummy(x_sb[0][:, 0, :], 2)
         x_chunk(1)
-        dummy(x_sb[1][:, 0, :], 2)
-        w_prep(1, (("V", 0, 1), ("G", 1, 3), ("S", 3, 4)))
         group1(0)
         x_chunk(2)
         group1(1)

@@ -216,7 +216,10 @@ def tile_selfattention_pa_kernel(tc, audio_feature, W_phi, b_phi, W_theta, b_the
                 )
 
         def mirror(g, jp, on_vector):
-            pt = ps_b.tile([P, 2, 2, P], F32, tag="B", name="pt")
+            if g >= 2:
+                pt = ps_a.tile([P, 2, 2, P], F32, tag="A", name="pt")
+            else:
+                pt = ps_b.tile([P, 2, 2, P], F32, tag="B", name="pt")
             for jj in range(2):
                 for ii in range(2):
                     t_sb, off = t_loc[(2 * g + ii, 2 * jp + jj)]

@@ -105,7 +105,7 @@ def tile_selfattention_pa_kernel(tc, audio_feature, W_phi, b_phi, W_theta, b_the
             hs.append(t_hs)
 
         def x_chunk(ch):
-            xt = ps_a.tile([P, 2, 2, P], F32, tag="A", name="xt")
+            xt = ps_b.tile([P, 2, 2, P], F32, tag="B", name="xt")
             for n2 in range(2):
                 words = x_sb[ch][:, n2, :].bitcast(F32)
                 for u in range(2):

from contextlib import ExitStack

import math

import concourse.mybir as mybir
from concourse.masks import make_identity

TOK, D_IN, HID = 1024, 512, 512
FLOPS = 2 * TOK * D_IN * HID * 2 + 2 * TOK * TOK * HID

F32 = mybir.dt.float32
BF16 = mybir.dt.bfloat16
U32 = mybir.dt.uint32
U8 = mybir.dt.uint8
FP8X4 = mybir.dt.float8_e4m3fn_x4
ACT = mybir.ActivationFunctionType
ALU = mybir.AluOpType

P = 128
PACK = 4
NT = TOK // P
BANK_DT = BF16
OUT_SCALE = 0.5 / math.sqrt(D_IN)
N_HEAT = 4


def tile_selfattention_pa_kernel(tc, audio_feature, W_phi, b_phi, W_theta, b_theta, out):
    nc = tc.nc
    x = audio_feature.flatten_outer_dims()
    o2 = out.flatten_outer_dims()
    w_dram = (W_theta, W_phi)
    b_dram = (b_theta, b_phi)

    with ExitStack() as ctx:
        keep = ctx.enter_context(tc.tile_pool(name="keep", bufs=1))
        work = ctx.enter_context(tc.tile_pool(name="work", bufs=3))
        ps_a = ctx.enter_context(tc.psum_pool(name="ps_a", bufs=3))
        ps_b = ctx.enter_context(tc.psum_pool(name="ps_b", bufs=5))

        b_raw = []
        for w in range(2):
            br = keep.tile([P, PACK], BF16, name="b_raw%d" % w)
            nc.scalar.dma_start(out=br[:], in_=b_dram[w].rearrange("(p t) -> p t", t=PACK))
            b_raw.append(br)

        w_raw = []
        x_sb = []
        for w in range(2):
            wr = keep.tile([P, PACK, HID], BF16, name="w_raw%d" % w)
            w_raw.append(wr)
        for ch in range(4):
            xc = keep.tile([P, 2, D_IN], BF16, name="x_sb%d" % ch)
            x_sb.append(xc)

        def load_w(w):
            nc.sync.dma_start(out=w_raw[w][:], in_=w_dram[w].rearrange("(p j) c -> p j c", j=PACK))

        def load_x(ch):
            nc.sync.dma_start(
                out=x_sb[ch][:],
                in_=x[2 * P * ch : 2 * P * (ch + 1), :].rearrange("(n p) k -> p n k", p=P),
            )

        load_w(0)
        load_w(1)
        load_x(0)
        load_x(1)
        load_x(2)
        load_x(3)

        ident = keep.tile([P, P], F32, name="ident")
        make_identity(nc, ident[:])
        zero1 = keep.tile([P, 1], F32, name="zero1")
        warm1 = keep.tile([P, 1], F32, name="warm1")
        nc.vector.memset(zero1[:], 0.0)
        nc.scalar.activation(out=warm1[:], in_=zero1[:], func=ACT.Relu)
        bias = b_raw

        heat = keep.tile([P, 512], BF16, name="heat")
        nc.vector.memset(heat[:], 0.0)
        hot = ps_b.tile([P, 512], F32, tag="B", name="hot")

        def dummy(moving, times):
            for rep in range(times):
                nc.tensor.matmul(out=hot[:], lhsT=heat[:, :P], rhs=moving, start=True, stop=True)

        dummy(heat[:], N_HEAT)

        xg = keep.tile([P, TOK * PACK], BF16, name="xg", align_bytes=64)
        xq = keep.tile([P, TOK], U32, name="xq", align_bytes=64)
        xs = keep.tile([P, TOK], U8, name="xs", align_bytes=64)
        wg, wq, ws, hg, hq, hs = [], [], [], [], [], []
        for w in range(2):
            t_wg = keep.tile([P, HID * PACK], BF16, name="wg%d" % w, align_bytes=64)
            t_wq = keep.tile([P, HID], U32, name="wq%d" % w, align_bytes=64)
            t_ws = keep.tile([P, HID], U8, name="ws%d" % w, align_bytes=64)
            t_hg = keep.tile([P, TOK * PACK], BF16, name="hg%d" % w, align_bytes=64)
            t_hq = keep.tile([P, TOK], U32, name="hq%d" % w, align_bytes=64)
            t_hs = keep.tile([P, TOK], U8, name="hs%d" % w, align_bytes=64)
            wg.append(t_wg)
            wq.append(t_wq)
            ws.append(t_ws)
            hg.append(t_hg)
            hq.append(t_hq)
            hs.append(t_hs)

        def x_chunk(ch):
            xt = ps_b.tile([P, 2, 2, P], F32, tag="B", name="xt")
            for n2 in range(2):
                words = x_sb[ch][:, n2, :].bitcast(F32)
                for u in range(2):
                    nc.tensor.transpose(xt[:, n2, u, :], words[:, u : D_IN // 2 : 2], ident[:])
            nc.scalar.copy(
                out=xg[:, 1024 * ch : 1024 * (ch + 1)].bitcast(F32).rearrange("p (n r u) -> p n r u", n=2, u=2),
                in_=xt[:].rearrange("p n u r -> p n r u"),
            )
            nc.vector.quantize_mx(
                out=xq[:, 256 * ch : 256 * (ch + 1)].bitcast(FP8X4),
                scales=xs[:, 256 * ch : 256 * (ch + 1)],
                in_=xg[:, 1024 * ch : 1024 * (ch + 1)],
            )

        def w_prep(w, shares):
            dst = wg[w][:].rearrange("p (t m j) -> p t m j", t=PACK, j=PACK)
            src = w_raw[w][:].rearrange("p j (m t) -> p t m j", t=PACK)
            for eng, t0, t1 in shares:
                if eng == "G":
                    nc.gpsimd.tensor_scalar(
                        out=dst[:, t0:t1], in0=src[:, t0:t1], scalar1=1.0, scalar2=0.0, op0=ALU.mult, op1=ALU.add
                    )
                elif eng == "S":
                    nc.scalar.copy(out=dst[:, t0:t1], in_=src[:, t0:t1])
                else:
                    nc.vector.tensor_copy(out=dst[:, t0:t1], in_=src[:, t0:t1])
            nc.vector.quantize_mx(out=wq[w][:].bitcast(FP8X4), scales=ws[w][:], in_=wg[w][:])

        def unit(w, m):
            ps1 = ps_a.tile([P, PACK, 2 * P], BANK_DT, tag="A", name="ps1")
            for t in range(PACK):
                nc.tensor.matmul_mx(
                    out=ps1[:, t, :],
                    lhsT=wq[w][:, P * t : P * (t + 1)].bitcast(FP8X4),
                    lhsT_scale=ws[w][:, P * t : P * (t + 1)],
                    rhs=xq[:, 256 * m : 256 * (m + 1)].bitcast(FP8X4),
                    rhs_scale=xs[:, 256 * m : 256 * (m + 1)],
                    start=True,
                    stop=True,
                )
            dst = hg[w][:, 1024 * m : 1024 * (m + 1)].rearrange("p (r t) -> p r t", t=PACK)
            if w == 0 and m > 0:
                lin = work.tile([P, PACK, 2 * P], BF16, tag="lin", name="lin", bufs=3)
                for t in range(PACK):
                    nc.scalar.activation(
                        out=lin[:, t, :], in_=ps1[:, t, :], func=ACT.Identity, bias=bias[w][:, t : t + 1], scale=1.0
                    )
                nc.gpsimd.tensor_scalar(
                    out=dst, in0=lin[:].rearrange("p t r -> p r t"), scalar1=1.0, scalar2=0.0, op0=ALU.mult, op1=ALU.add
                )
            else:
                nc.vector.tensor_tensor(
                    out=dst,
                    in0=ps1[:].rearrange("p t r -> p r t"),
                    in1=bias[w][:].unsqueeze(1).to_broadcast([P, 2 * P, PACK]),
                    op=ALU.add,
                )

        def quant_pair(w, m):
            nc.vector.quantize_mx(
                out=hq[w][:, 256 * m : 256 * (m + 1)].bitcast(FP8X4),
                scales=hs[w][:, 256 * m : 256 * (m + 1)],
                in_=hg[w][:, 1024 * m : 1024 * (m + 1)],
            )

        def mx2(dst, wl, i, wr, col0, width):
            nc.tensor.matmul_mx(
                out=dst,
                lhsT=hq[wl][:, P * i : P * (i + 1)].bitcast(FP8X4),
                lhsT_scale=hs[wl][:, P * i : P * (i + 1)],
                rhs=hq[wr][:, col0 : col0 + width].bitcast(FP8X4),
                rhs_scale=hs[wr][:, col0 : col0 + width],
                start=True,
                stop=True,
            )

        t_loc = {}

        def direct(pieces, on_vector):
            pa = ps_b.tile([P, 512], F32, tag="B", name="pa")
            pb = ps_b.tile([P, 512], F32, tag="B", name="pb")
            t_sb = keep.tile([P, 512], F32, name="t_sb%d_%d" % (pieces[0][0], pieces[0][1]))
            off = 0
            for i, col0, width in pieces:
                mx2(pa[:, off : off + width], 1, i, 0, col0, width)
                for b in range(width // P):
                    t_loc[(i, col0 // P + b)] = (t_sb, off + P * b)
                off += width
            off = 0
            for i, col0, width in pieces:
                mx2(pb[:, off : off + width], 0, i, 1, col0, width)
                off += width
            a_sb = work.tile([P, 512], F32, tag="a_sb", name="a_sb", bufs=4)
            o_sb = work.tile([P, 512], F32, tag="o_sb", name="o_sb", bufs=12)
            nc.scalar.activation(out=a_sb[:], in_=pa[:], func=ACT.Relu)
            nc.vector.scalar_tensor_tensor(out=t_sb[:], in0=pb[:], scalar=0.0, in1=a_sb[:], op0=ALU.max, op1=ALU.add)
            if on_vector:
                nc.vector.tensor_scalar_mul(out=o_sb[:], in0=t_sb[:], scalar1=OUT_SCALE)
            else:
                nc.gpsimd.tensor_scalar(out=o_sb[:], in0=t_sb[:], scalar1=OUT_SCALE, scalar2=0.0, op0=ALU.mult, op1=ALU.add)
            i, col0, width = pieces[0]
            if len(pieces) == 1:
                nc.sync.dma_start(out=o2[P * i : P * (i + 1), col0 : col0 + width], in_=o_sb[:])
            else:
                nc.sync.dma_start(
                    out=o2[P * i : P * (i + 2), col0 : col0 + width].rearrange("(a p) c -> p a c", p=P),
                    in_=o_sb[:].rearrange("p (a c) -> p a c", a=2),
                )

        def mirror(g, jp, on_vector):
            if g >= 2:
                pt = ps_a.tile([P, 2, 2, P], F32, tag="A", name="pt")
            else:
                pt = ps_b.tile([P, 2, 2, P], F32, tag="B", name="pt")
            for jj in range(2):
                for ii in range(2):
                    t_sb, off = t_loc[(2 * g + ii, 2 * jp + jj)]
                    nc.tensor.transpose(pt[:, jj, ii, :], t_sb[:, off : off + P], ident[:])
            m_sb = work.tile([P, 2, 2 * P], F32, tag="o_sb", name="m_sb", bufs=12)
            flat = pt[:].rearrange("p a b r -> p (a b r)")
            if on_vector:
                nc.vector.tensor_scalar_mul(out=m_sb[:].rearrange("p a c -> p (a c)"), in0=flat, scalar1=OUT_SCALE)
            else:
                nc.scalar.activation(out=m_sb[:].rearrange("p a c -> p (a c)"), in_=flat, func=ACT.Copy, scale=OUT_SCALE)
            queue = nc.sync if on_vector else nc.scalar
            queue.dma_start(
                out=o2[256 * jp : 256 * (jp + 1), 256 * g : 256 * (g + 1)].rearrange("(a p) c -> p a c", p=P),
                in_=m_sb[:],
            )

        def group1(g):
            unit(0, g)
            unit(1, g)
            quant_pair(1, g)
            quant_pair(0, g)

        def stage2(g):
            rows = (2 * g, 2 * g + 1)
            last = g == NT // 2 - 1
            for col0 in range(0, 512 * (g // 2), 512):
                for i in rows:
                    direct(((i, col0, 512),), False)
            if g % 2 == 1 and not last:
                for i in rows:
                    direct(((i, 256 * (g - 1), 512),), False)
            if g % 2 == 1 and last:
                direct(tuple((i, 256 * (g - 1), 256) for i in rows), False)
            if g % 2 == 0 or last:
                direct(tuple((i, 256 * g, 256) for i in rows), last)
            for jp in range(g):
                mirror(g, jp, jp % 2 == 1)

        dummy(w_raw[0][:, 0, :], 2)
        w_prep(0, (("V", 0, 2), ("S", 2, 4)))
        dummy(w_raw[1][:, 0, :], 2)
        w_prep(1, (("V", 0, 2), ("S", 2, 4)))
        x_chunk(0)
        dummy(x_sb[0][:, 0, :], 2)
        x_chunk(1)
        group1(0)
        x_chunk(2)
        group1(1)
        stage2(0)
        x_chunk(3)
        group1(2)
        stage2(1)
        group1(3)
        stage2(2)
        stage2(3)
